import numpy as np
import ml_dtypes


def mxq(x, axis, fmt="e4m3"):
    dtype, down = {"e4m3": (ml_dtypes.float8_e4m3fn, 7), "e5m2": (ml_dtypes.float8_e5m2, 14)}[fmt]
    v = np.moveaxis(np.asarray(x, np.float32).astype(ml_dtypes.bfloat16).astype(np.float64), axis, -1)
    blocks = v.reshape(v.shape[:-1] + (-1, 32))
    amax = np.abs(blocks).max(-1, keepdims=True)
    byte = np.maximum(np.where(amax > 0, np.frexp(amax)[1] - 1 + 127, 0) - down, 1)
    scale = np.exp2(byte - 127.0)
    codes = (blocks / scale).astype(np.float32).astype(dtype).astype(np.float64)
    return np.moveaxis((codes * scale).reshape(v.shape), -1, axis)


WIDE = False


def mx_kscale(k):
    if not WIDE:
        return np.ones(k)
    levels = np.array([10, -10, 5, -5, 0])
    a = np.random.permutation(np.resize(levels, k // 512 * 4)).reshape(k // 512, 4)
    idx = np.arange(k)
    return np.exp2(a[idx // 512, idx % 128 // 32])


BF16 = ml_dtypes.bfloat16


def bf(x):
    return np.asarray(x, np.float32).astype(BF16)


def f64(x):
    return np.asarray(x).astype(np.float64)


B, T, DX, DY, F = 128, 8, 1024, 1024, 5
MIN_CONTEXT = 1
G = 1.5 / DY ** 0.25


def setup_inputs():
    s, t = mx_kscale(DX), mx_kscale(DY)
    return {"embeddings": bf(np.random.standard_normal((B, T, DX)) * s),
            "contexts": bf(np.random.standard_normal((B, T, DY)) * G / t),
            "W": bf(np.random.standard_normal((F, DY, DX)) * G / np.sqrt(DX) * t[:, None] / s)}


def reference(embeddings, contexts, W):
    eq = mxq(f64(embeddings)[:, MIN_CONTEXT:T], 2, "e4m3")
    cq = mxq(f64(contexts)[:, MIN_CONTEXT - 1:T - 1], 2, "e4m3")
    wq = mxq(f64(W), 2, "e4m3")
    losses = []
    for step in range(F):
        S = T - step - MIN_CONTEXT
        xw = eq[:, step:] @ wq[step].T
        scores = mxq(xw, 2, "e4m3").transpose(1, 0, 2) @ cq[:, :S].transpose(1, 2, 0)
        pos = np.diagonal(scores, axis1=1, axis2=2)
        m = scores.max(2, keepdims=True)
        lse = np.log(np.exp(scores - m).sum(2)) + m[:, :, 0] - np.log(B * S)
        losses.append((lse - pos).T.reshape(-1))
    return np.concatenate(losses)

@@ -1,0 +1,283 @@
+from contextlib import ExitStack
+
+import concourse.mybir as mybir
+from concourse.masks import make_identity
+
+F32 = mybir.dt.float32
+BF16 = mybir.dt.bfloat16
+U32 = mybir.dt.uint32
+U8 = mybir.dt.uint8
+FP8X4 = mybir.dt.float8_e4m3fn_x4
+ALU = mybir.AluOpType
+ACT = mybir.ActivationFunctionType
+AX = mybir.AxisListType
+
+P = 128
+FEAT = 1024
+N_STEP = 5
+N_SLICE = 7
+GROUP0 = [0, 7, 13, 18, 22]
+N_GROUP = 25
+B_LO = 8
+B_HI = 16
+FLOPS = 2 * N_GROUP * P * FEAT * FEAT + 2 * N_GROUP * P * P * FEAT
+
+PINNED = False
+
+
+def tile_infonceloss_pa_kernel(tc, embeddings, contexts, W, out):
+    nc = tc.nc
+    with ExitStack() as ctx:
+        const = ctx.enter_context(tc.tile_pool(name="const", bufs=1))
+        raw = ctx.enter_context(tc.tile_pool(name="raw", bufs=1))
+        wraw_pool = ctx.enter_context(tc.tile_pool(name="wraw", bufs=7))
+        grp_pool = ctx.enter_context(tc.tile_pool(name="grp", bufs=3))
+        keep = ctx.enter_context(tc.tile_pool(name="keep", bufs=1))
+        xwg_pool = ctx.enter_context(tc.tile_pool(name="xwg", bufs=4))
+        junk = ctx.enter_context(tc.tile_pool(name="junk", bufs=2))
+        ring = ctx.enter_context(tc.psum_pool(name="ring", bufs=6))
+        scp = ctx.enter_context(tc.psum_pool(name="scores", bufs=2))
+        if PINNED:
+            ctx.enter_context(tc.manual_schedule())
+
+        x_raw = raw.tile([P, N_SLICE, FEAT], BF16, name="x_raw")
+        c_raw = raw.tile([P, N_SLICE, FEAT], BF16, name="c_raw")
+        w_raw = {}
+
+        def load_x(t0, t1):
+            nc.sync.dma_start(out=x_raw[:, t0:t1, :], in_=embeddings[:, 1 + t0 : 1 + t1, :])
+
+        def load_c(t0, t1):
+            nc.sync.dma_start(out=c_raw[:, t0:t1, :], in_=contexts[:, t0:t1, :])
+
+        def load_w(k, g):
+            t = wraw_pool.tile([P, 4, FEAT], BF16, name="w_raw", tag="w_raw")
+            nc.sync.dma_start(
+                out=t[:].rearrange("p (u e) d -> p u (e d)", e=2),
+                in_=W[k, 512 * g : 512 * (g + 1), :].rearrange("(u p e) d -> p u (e d)", u=2, e=2),
+            )
+            w_raw[(k, g)] = t
+
+        load_x(0, 4)
+        load_w(0, 0)
+        load_x(4, 7)
+        load_w(0, 1)
+        load_w(1, 0)
+        load_c(0, 4)
+        load_w(1, 1)
+        load_c(4, 7)
+        load_w(2, 0)
+        load_w(2, 1)
+        load_w(3, 0)
+
+        ident = const.tile([P, P], F32, name="ident")
+        make_identity(nc, ident[:])
+        warm = const.tile([P, 2], F32, name="warm")
+        nc.vector.memset(warm[:], 1.0)
+        nc.scalar.activation(out=warm[:, 1:2], in_=warm[:, 0:1], func=ACT.Exp)
+        mask8 = const.tile([P, B_LO], F32, name="mask8")
+        nc.vector.tensor_reduce(
+            out=mask8[:], in_=ident[:].rearrange("p (q l) -> p l q", l=B_LO), axis=AX.X, op=ALU.add
+        )
+        fold = const.tile([P, P], F32, name="fold")
+        nc.vector.memset(fold[:], 0.0)
+        nc.vector.tensor_reduce(
+            out=fold[:, 0:B_HI], in_=ident[:].rearrange("p (q l) -> p q l", l=B_LO), axis=AX.X, op=ALU.add
+        )
+
+        xq = keep.tile([P, N_SLICE, 256], U32, name="xq", align_bytes=64)
+        xs = keep.tile([P, N_SLICE, 256], U8, name="xs", align_bytes=64)
+        cq = keep.tile([P, N_SLICE, 256], U32, name="cq", align_bytes=64)
+        cs = keep.tile([P, N_SLICE, 256], U8, name="cs", align_bytes=64)
+        wq = [keep.tile([P, 8, 256], U32, name="wq%d" % k, align_bytes=64) for k in range(N_STEP)]
+        ws = [keep.tile([P, 8, 256], U8, name="ws%d" % k, align_bytes=64) for k in range(N_STEP)]
+        xwq = keep.tile([P, 2 * N_GROUP, P], U32, name="xwq", align_bytes=64)
+        xws = keep.tile([P, 2 * N_GROUP, P], U8, name="xws", align_bytes=64)
+        negmax = keep.tile([P, N_GROUP], F32, name="negmax")
+        sumexp = keep.tile([P, N_GROUP], F32, name="sumexp")
+        dm = keep.tile([P, N_GROUP], F32, name="dm")
+        spread_s = keep.tile([P, B_LO * N_GROUP], F32, name="spread_s")
+        spread_d = keep.tile([P, B_LO * N_GROUP], F32, name="spread_d")
+
+        def flat(ap):
+            return ap.rearrange("p i c -> p (i c)")
+
+        def quantise(codes, scales, values):
+            nc.vector.quantize_mx(out=flat(codes).bitcast(FP8X4), scales=flat(scales), in_=flat(values))
+
+        def prep(rows, codes, scales):
+            n = len(rows)
+            grp = grp_pool.tile([P, 4, FEAT], BF16, name="grp", tag="grp", align_bytes=64)
+            for i in range(n):
+                bank = ring.tile([P, 4, P], F32, name="bank", tag="bank")
+                words = rows[i].bitcast(F32)
+                for j in range(4):
+                    nc.tensor.transpose(bank[:, j, :], words[:, P * j : P * (j + 1)], ident[:])
+                dst = grp[:, i, :].bitcast(F32).rearrange("p (g r u) -> p g r u", g=2, u=2)
+                src = bank[:].rearrange("p (g u) r -> p g r u", u=2)
+                if i % 2 == 0:
+                    nc.vector.tensor_copy(out=dst, in_=src)
+                else:
+                    nc.scalar.copy(out=dst, in_=src)
+            i0 = 0
+            for width in (4, 2, 1):
+                if n - i0 >= width:
+                    quantise(codes[:, i0 : i0 + width, :], scales[:, i0 : i0 + width, :], grp[:, i0 : i0 + width, :])
+                    i0 += width
+
+        def prep_x(t0, t1):
+            prep([x_raw[:, t, :] for t in range(t0, t1)], xq[:, t0:t1, :], xs[:, t0:t1, :])
+
+        def prep_c(t0, t1):
+            prep([c_raw[:, t, :] for t in range(t0, t1)], cq[:, t0:t1, :], cs[:, t0:t1, :])
+
+        def prep_w(k, g):
+            t = w_raw[(k, g)]
+            prep([t[:, j, :] for j in range(4)], wq[k][:, 4 * g : 4 * g + 4, :], ws[k][:, 4 * g : 4 * g + 4, :])
+
+        def xw_row(k, g2, s):
+            return 2 * GROUP0[k] + g2 * (N_SLICE - k) + s
+
+        def stage1(k, g2, s_list):
+            for c0 in range(0, len(s_list), 2):
+                chunk = s_list[c0 : c0 + 2]
+                n = len(chunk)
+                xwg = xwg_pool.tile([P, 2, 512], BF16, name="xwg", tag="xwg", align_bytes=64)
+                for i in range(n):
+                    s = chunk[i]
+                    bank = ring.tile([P, 4, P], F32, name="bank", tag="bank")
+                    for t in range(4):
+                        for g1 in range(2):
+                            cols = slice(P * g1, P * (g1 + 1))
+                            nc.tensor.matmul_mx(
+                                out=bank[:, t, :],
+                                lhsT=wq[k][:, 4 * g2 + t, cols].bitcast(FP8X4),
+                                lhsT_scale=ws[k][:, 4 * g2 + t, cols],
+                                rhs=xq[:, k + s, cols].bitcast(FP8X4),
+                                rhs_scale=xs[:, k + s, cols],
+                                start=(g1 == 0),
+                                stop=(g1 == 1),
+                            )
+                    nc.scalar.copy(
+                        out=xwg[:, i, :].rearrange("p (b t) -> p b t", t=4),
+                        in_=bank[:].rearrange("p t b -> p b t"),
+                    )
+                r0 = xw_row(k, g2, chunk[0])
+                quantise(xwq[:, r0 : r0 + n, :], xws[:, r0 : r0 + n, :], xwg[:, 0:n, :])
+
+        def stage2(k):
+            n_s = N_SLICE - k
+            for s0 in range(0, n_s, 4):
+                n = min(4, n_s - s0)
+                sc = scp.tile([P, 4, P], F32, name="sc", tag="sc")
+                for i in range(n):
+                    s = s0 + i
+                    for g2 in range(2):
+                        r = xw_row(k, g2, s)
+                        cols = slice(P * g2, P * (g2 + 1))
+                        nc.tensor.matmul_mx(
+                            out=sc[:, i, :],
+                            lhsT=xwq[:, r, :].bitcast(FP8X4),
+                            lhsT_scale=xws[:, r, :],
+                            rhs=cq[:, s, cols].bitcast(FP8X4),
+                            rhs_scale=cs[:, s, cols],
+                            start=(g2 == 0),
+                            stop=(g2 == 1),
+                        )
+                gi = GROUP0[k] + s0
+                nc.vector.tensor_reduce(
+                    out=negmax[:, gi : gi + n], in_=sc[:, 0:n, :], axis=AX.X, op=ALU.max, negate=True
+                )
+                for i in range(n):
+                    jv = junk.tile([P, P], F32, name="jv", tag="jv")
+                    nc.vector.scalar_tensor_tensor(
+                        out=jv[:],
+                        in0=sc[:, i, :],
+                        scalar=negmax[:, gi + i : gi + i + 1],
+                        in1=ident[:],
+                        op0=ALU.add,
+                        op1=ALU.mult,
+                        accum_out=dm[:, gi + i : gi + i + 1],
+                    )
+                for i in range(n):
+                    js = junk.tile([P, P], F32, name="js", tag="js")
+                    nc.scalar.activation(
+                        out=js[:],
+                        in_=sc[:, i, :],
+                        func=ACT.Exp,
+                        bias=negmax[:, gi + i : gi + i + 1],
+                        scale=1.0,
+                        accum_out=sumexp[:, gi + i : gi + i + 1],
+                    )
+            g0 = GROUP0[k]
+            shape = [P, B_LO, n_s]
+            mask = mask8[:].unsqueeze(2).to_broadcast(shape)
+            cols = slice(B_LO * g0, B_LO * (g0 + n_s))
+            nc.vector.tensor_tensor(
+                out=spread_d[:, cols].rearrange("p (l s) -> p l s", l=B_LO),
+                in0=dm[:, g0 : g0 + n_s].unsqueeze(1).to_broadcast(shape),
+                in1=mask,
+                op=ALU.mult,
+            )
+            nc.vector.scalar_tensor_tensor(
+                out=spread_s[:, cols].rearrange("p (l s) -> p l s", l=B_LO),
+                in0=sumexp[:, g0 : g0 + n_s].unsqueeze(1).to_broadcast(shape),
+                scalar=1.0 / (P * n_s),
+                in1=mask,
+                op0=ALU.mult,
+                op1=ALU.mult,
+            )
+
+        prep_x(0, 4)
+        prep_w(0, 0)
+        load_w(3, 1)
+        prep_x(4, 7)
+        stage1(0, 0, [0, 1, 2, 3])
+        prep_w(0, 1)
+        load_w(4, 0)
+        stage1(0, 0, [4, 5, 6])
+        prep_w(1, 0)
+        load_w(4, 1)
+        stage1(0, 1, [0, 1, 2, 3])
+        prep_c(0, 4)
+        stage1(0, 1, [4, 5, 6])
+        prep_w(1, 1)
+        stage1(1, 0, [0, 1, 2])
+        prep_c(4, 7)
+        stage1(1, 0, [3, 4, 5])
+        prep_w(2, 0)
+        stage2(0)
+        stage1(1, 1, [0, 1, 2, 3, 4, 5])
+        prep_w(2, 1)
+        stage2(1)
+        stage1(2, 0, [0, 1, 2, 3, 4])
+        prep_w(3, 0)
+        stage1(2, 1, [0, 1, 2, 3, 4])
+        prep_w(3, 1)
+        stage2(2)
+        stage1(3, 0, [0, 1, 2, 3])
+        prep_w(4, 0)
+        stage1(3, 1, [0, 1, 2, 3])
+        prep_w(4, 1)
+        stage2(3)
+        stage1(4, 0, [0, 1, 2])
+        stage1(4, 1, [0, 1, 2])
+        stage2(4)
+
+        n_col = B_LO * N_GROUP
+        nc.scalar.activation(out=warm[:, 1:2], in_=sumexp[:, N_GROUP - 1 : N_GROUP], func=ACT.Ln)
+        zd = ring.tile([P, 512], F32, name="zd", tag="bank")
+        nc.tensor.matmul(zd[:, 0:n_col], lhsT=fold[:], rhs=spread_d[:], start=True, stop=True)
+        zs = ring.tile([P, 512], F32, name="zs", tag="bank")
+        nc.tensor.matmul(zs[:, 0:n_col], lhsT=fold[:], rhs=spread_s[:], start=True, stop=True)
+        lnz = keep.tile([P, n_col], F32, name="lnz")
+        nc.scalar.activation(out=lnz[0:B_HI, :], in_=zs[0:B_HI, 0:n_col], func=ACT.Ln)
+        res = keep.tile([P, n_col], F32, name="res")
+        nc.vector.tensor_tensor(out=res[0:B_HI, :], in0=lnz[0:B_HI, :], in1=zd[0:B_HI, 0:n_col], op=ALU.subtract)
+        for k in range(N_STEP):
+            n_s = N_SLICE - k
+            g0 = GROUP0[k]
+            nc.sync.dma_start(
+                out=out[P * g0 : P * (g0 + n_s)].rearrange("(q c) -> q c", q=B_HI),
+                in_=res[0:B_HI, B_LO * g0 : B_LO * (g0 + n_s)],
+            )

@@ -22,7 +22,9 @@ B_LO = 8
 B_HI = 16
 FLOPS = 2 * N_GROUP * P * FEAT * FEAT + 2 * N_GROUP * P * P * FEAT
 
-PINNED = False
+QW = 2
+HALF = (1, 4, 7)
+PINNED = True
 
 
 def tile_infonceloss_pa_kernel(tc, embeddings, contexts, W, out):
@@ -31,7 +33,7 @@ def tile_infonceloss_pa_kernel(tc, embeddings, contexts, W, out):
         const = ctx.enter_context(tc.tile_pool(name="const", bufs=1))
         raw = ctx.enter_context(tc.tile_pool(name="raw", bufs=1))
         wraw_pool = ctx.enter_context(tc.tile_pool(name="wraw", bufs=7))
-        grp_pool = ctx.enter_context(tc.tile_pool(name="grp", bufs=3))
+        grp_pool = ctx.enter_context(tc.tile_pool(name="grp", bufs=4))
         keep = ctx.enter_context(tc.tile_pool(name="keep", bufs=1))
         xwg_pool = ctx.enter_context(tc.tile_pool(name="xwg", bufs=4))
         junk = ctx.enter_context(tc.tile_pool(name="junk", bufs=2))
@@ -50,21 +52,24 @@ def tile_infonceloss_pa_kernel(tc, embeddings, contexts, W, out):
         def load_c(t0, t1):
             nc.sync.dma_start(out=c_raw[:, t0:t1, :], in_=contexts[:, t0:t1, :])
 
-        def load_w(k, g):
+        def load_w(k, g, pieces=1):
             t = wraw_pool.tile([P, 4, FEAT], BF16, name="w_raw", tag="w_raw")
-            nc.sync.dma_start(
-                out=t[:].rearrange("p (u e) d -> p u (e d)", e=2),
-                in_=W[k, 512 * g : 512 * (g + 1), :].rearrange("(u p e) d -> p u (e d)", u=2, e=2),
-            )
+            dst = t[:].rearrange("p (u e) d -> p u (e d)", e=2)
+            src = W[k, 512 * g : 512 * (g + 1), :].rearrange("(u p e) d -> p u (e d)", u=2, e=2)
+            step = 2 // pieces
+            for u in range(0, 2, step):
+                nc.sync.dma_start(out=dst[:, u : u + step, :], in_=src[:, u : u + step, :])
             w_raw[(k, g)] = t
 
-        load_x(0, 4)
-        load_w(0, 0)
+        load_x(0, 1)
+        load_w(0, 0, 2)
+        load_x(1, 2)
+        load_x(2, 4)
         load_x(4, 7)
         load_w(0, 1)
         load_w(1, 0)
-        load_c(0, 4)
         load_w(1, 1)
+        load_c(0, 4)
         load_c(4, 7)
         load_w(2, 0)
         load_w(2, 1)
@@ -99,13 +104,42 @@ def tile_infonceloss_pa_kernel(tc, embeddings, contexts, W, out):
         spread_s = keep.tile([P, B_LO * N_GROUP], F32, name="spread_s")
         spread_d = keep.tile([P, B_LO * N_GROUP], F32, name="spread_d")
 
+        urgent = []
+        urgent_done = [0]
+        backlog = []
+        backlog_done = [0]
+        ready_at = {}
+
+        def next_job():
+            if urgent_done[0] < len(urgent):
+                urgent[urgent_done[0]]()
+                urgent_done[0] += 1
+            elif backlog_done[0] < len(backlog):
+                backlog[backlog_done[0]]()
+                backlog_done[0] += 1
+
+        def need(key):
+            for i in range(backlog_done[0], ready_at.get(key, 0)):
+                backlog[i]()
+            backlog_done[0] = max(backlog_done[0], ready_at.get(key, 0))
+
+        def flush_jobs():
+            for i in range(urgent_done[0], len(urgent)):
+                urgent[i]()
+            urgent_done[0] = len(urgent)
+            for i in range(backlog_done[0], len(backlog)):
+                backlog[i]()
+            backlog_done[0] = len(backlog)
+
         def flat(ap):
             return ap.rearrange("p i c -> p (i c)")
 
         def quantise(codes, scales, values):
             nc.vector.quantize_mx(out=flat(codes).bitcast(FP8X4), scales=flat(scales), in_=flat(values))
 
-        def prep(rows, codes, scales):
+        turn = [0]
+
+        def prep(rows, codes, scales, now, vector_share):
             n = len(rows)
             grp = grp_pool.tile([P, 4, FEAT], BF16, name="grp", tag="grp", align_bytes=64)
             for i in range(n):
@@ -115,32 +149,43 @@ def tile_infonceloss_pa_kernel(tc, embeddings, contexts, W, out):
                     nc.tensor.transpose(bank[:, j, :], words[:, P * j : P * (j + 1)], ident[:])
                 dst = grp[:, i, :].bitcast(F32).rearrange("p (g r u) -> p g r u", g=2, u=2)
                 src = bank[:].rearrange("p (g u) r -> p g r u", u=2)
-                if i % 2 == 0:
+                if turn[0] % 8 in vector_share:
                     nc.vector.tensor_copy(out=dst, in_=src)
                 else:
                     nc.scalar.copy(out=dst, in_=src)
-            i0 = 0
-            for width in (4, 2, 1):
-                if n - i0 >= width:
-                    quantise(codes[:, i0 : i0 + width, :], scales[:, i0 : i0 + width, :], grp[:, i0 : i0 + width, :])
-                    i0 += width
+                turn[0] += 1
+            for i0 in range(0, n, QW):
+                w = min(QW, n - i0)
+                assert w in (1, 2, 4)
+                job = job_quantise(codes[:, i0 : i0 + w, :], scales[:, i0 : i0 + w, :], grp[:, i0 : i0 + w, :])
+                if now:
+                    job()
+                else:
+                    backlog.append(job)
 
-        def prep_x(t0, t1):
-            prep([x_raw[:, t, :] for t in range(t0, t1)], xq[:, t0:t1, :], xs[:, t0:t1, :])
+        def job_quantise(codes, scales, values):
+            return lambda: quantise(codes, scales, values)
 
-        def prep_c(t0, t1):
-            prep([c_raw[:, t, :] for t in range(t0, t1)], cq[:, t0:t1, :], cs[:, t0:t1, :])
+        def prep_x(t0, t1, now=True, share=HALF):
+            prep([x_raw[:, t, :] for t in range(t0, t1)], xq[:, t0:t1, :], xs[:, t0:t1, :], now, share)
 
-        def prep_w(k, g):
+        def prep_c(t0, t1, now=False, share=HALF):
+            prep([c_raw[:, t, :] for t in range(t0, t1)], cq[:, t0:t1, :], cs[:, t0:t1, :], now, share)
+            ready_at["c"] = len(backlog)
+
+        def prep_w(k, g, now=False, share=HALF):
             t = w_raw[(k, g)]
-            prep([t[:, j, :] for j in range(4)], wq[k][:, 4 * g : 4 * g + 4, :], ws[k][:, 4 * g : 4 * g + 4, :])
+            prep([t[:, j, :] for j in range(4)], wq[k][:, 4 * g : 4 * g + 4, :], ws[k][:, 4 * g : 4 * g + 4, :], now, share)
+            ready_at[(k, g)] = len(backlog)
 
         def xw_row(k, g2, s):
             return 2 * GROUP0[k] + g2 * (N_SLICE - k) + s
 
-        def stage1(k, g2, s_list):
-            for c0 in range(0, len(s_list), 2):
-                chunk = s_list[c0 : c0 + 2]
+        def stage1(k, g2, chunks, vector_banks=(), per_slot=1):
+            need((k, g2))
+            for i in range(per_slot):
+                next_job()
+            for chunk in chunks:
                 n = len(chunk)
                 xwg = xwg_pool.tile([P, 2, 512], BF16, name="xwg", tag="xwg", align_bytes=64)
                 for i in range(n):
@@ -158,18 +203,35 @@ def tile_infonceloss_pa_kernel(tc, embeddings, contexts, W, out):
                                 start=(g1 == 0),
                                 stop=(g1 == 1),
                             )
-                    nc.scalar.copy(
-                        out=xwg[:, i, :].rearrange("p (b t) -> p b t", t=4),
-                        in_=bank[:].rearrange("p t b -> p b t"),
-                    )
+                    dst = xwg[:, i, :].rearrange("p (b t) -> p b t", t=4)
+                    src = bank[:].rearrange("p t b -> p b t")
+                    if s in vector_banks:
+                        nc.vector.tensor_copy(out=dst, in_=src)
+                    else:
+                        nc.scalar.copy(out=dst, in_=src)
                 r0 = xw_row(k, g2, chunk[0])
                 quantise(xwq[:, r0 : r0 + n, :], xws[:, r0 : r0 + n, :], xwg[:, 0:n, :])
+                for i in range(per_slot):
+                    next_job()
 
-        def stage2(k):
+        def pairs(n):
+            return [list(range(s, min(s + 2, n))) for s in range(0, n, 2)]
+
+        sc_banks = {}
+
+        def s2_matmuls(k, s0_list=(0, 4), pool=None):
+            need("c")
             n_s = N_SLICE - k
-            for s0 in range(0, n_s, 4):
-                n = min(4, n_s - s0)
-                sc = scp.tile([P, 4, P], F32, name="sc", tag="sc")
+            sc_banks[k] = []
+            for j in range(len(s0_list)):
+                s0 = s0_list[j]
+                if s0 >= n_s:
+                    continue
+                n = min(s0_list[j + 1] if j + 1 < len(s0_list) else n_s, n_s) - s0
+                if pool is None:
+                    sc = scp.tile([P, 4, P], F32, name="sc", tag="sc")
+                else:
+                    sc = pool.tile([P, 4, P], F32, name="bank", tag="bank")
                 for i in range(n):
                     s = s0 + i
                     for g2 in range(2):
@@ -184,92 +246,142 @@ def tile_infonceloss_pa_kernel(tc, embeddings, contexts, W, out):
                             start=(g2 == 0),
                             stop=(g2 == 1),
                         )
-                gi = GROUP0[k] + s0
+                sc_banks[k].append((sc, GROUP0[k] + s0, n))
+
+        def s2_max(k):
+            for sc, gi, n in sc_banks[k]:
                 nc.vector.tensor_reduce(
                     out=negmax[:, gi : gi + n], in_=sc[:, 0:n, :], axis=AX.X, op=ALU.max, negate=True
                 )
-                for i in range(n):
-                    jv = junk.tile([P, P], F32, name="jv", tag="jv")
-                    nc.vector.scalar_tensor_tensor(
-                        out=jv[:],
-                        in0=sc[:, i, :],
-                        scalar=negmax[:, gi + i : gi + i + 1],
-                        in1=ident[:],
-                        op0=ALU.add,
-                        op1=ALU.mult,
-                        accum_out=dm[:, gi + i : gi + i + 1],
-                    )
-                for i in range(n):
-                    js = junk.tile([P, P], F32, name="js", tag="js")
-                    nc.scalar.activation(
-                        out=js[:],
-                        in_=sc[:, i, :],
-                        func=ACT.Exp,
-                        bias=negmax[:, gi + i : gi + i + 1],
-                        scale=1.0,
-                        accum_out=sumexp[:, gi + i : gi + i + 1],
-                    )
+
+        def exps(k, b):
+            sc, gi, n = sc_banks[k][b]
+            for i in range(n):
+                js = junk.tile([P, P], F32, name="js", tag="js")
+                nc.scalar.activation(
+                    out=js[:],
+                    in_=sc[:, i, :],
+                    func=ACT.Exp,
+                    bias=negmax[:, gi + i : gi + i + 1],
+                    scale=1.0,
+                    accum_out=sumexp[:, gi + i : gi + i + 1],
+                )
+
+        def diag(k, b):
+            sc, gi, n = sc_banks[k][b]
+            for i in range(n):
+                jv = junk.tile([P, P], F32, name="jv", tag="jv")
+                nc.vector.scalar_tensor_tensor(
+                    out=jv[:],
+                    in0=sc[:, i, :],
+                    scalar=negmax[:, gi + i : gi + i + 1],
+                    in1=ident[:],
+                    op0=ALU.add,
+                    op1=ALU.mult,
+                    accum_out=dm[:, gi + i : gi + i + 1],
+                )
+
+        def spread_diag(k):
+            n_s = N_SLICE - k
             g0 = GROUP0[k]
             shape = [P, B_LO, n_s]
-            mask = mask8[:].unsqueeze(2).to_broadcast(shape)
-            cols = slice(B_LO * g0, B_LO * (g0 + n_s))
             nc.vector.tensor_tensor(
-                out=spread_d[:, cols].rearrange("p (l s) -> p l s", l=B_LO),
+                out=spread_d[:, B_LO * g0 : B_LO * (g0 + n_s)].rearrange("p (l s) -> p l s", l=B_LO),
                 in0=dm[:, g0 : g0 + n_s].unsqueeze(1).to_broadcast(shape),
-                in1=mask,
+                in1=mask8[:].unsqueeze(2).to_broadcast(shape),
                 op=ALU.mult,
             )
+
+        def spread_sum(k):
+            n_s = N_SLICE - k
+            g0 = GROUP0[k]
+            shape = [P, B_LO, n_s]
             nc.vector.scalar_tensor_tensor(
-                out=spread_s[:, cols].rearrange("p (l s) -> p l s", l=B_LO),
+                out=spread_s[:, B_LO * g0 : B_LO * (g0 + n_s)].rearrange("p (l s) -> p l s", l=B_LO),
                 in0=sumexp[:, g0 : g0 + n_s].unsqueeze(1).to_broadcast(shape),
                 scalar=1.0 / (P * n_s),
-                in1=mask,
+                in1=mask8[:].unsqueeze(2).to_broadcast(shape),
                 op0=ALU.mult,
                 op1=ALU.mult,
             )
 
-        prep_x(0, 4)
-        prep_w(0, 0)
+        def job_max_diag(k, b):
+            def job():
+                sc, gi, n = sc_banks[k][b]
+                nc.vector.tensor_reduce(
+                    out=negmax[:, gi : gi + n], in_=sc[:, 0:n, :], axis=AX.X, op=ALU.max, negate=True
+                )
+                diag(k, b)
+            return job
+
+        def job_spread(k):
+            def job():
+                spread_diag(k)
+                spread_sum(k)
+            return job
+
+        def all_exps(k):
+            for b in range(len(sc_banks[k])):
+                exps(k, b)
+            backlog.append(job_spread(k))
+
+        prep_x(0, 1)
+        prep_w(0, 0, True)
         load_w(3, 1)
+        prep_x(1, 2)
+        prep_x(2, 4)
+        stage1(0, 0, pairs(4))
         prep_x(4, 7)
-        stage1(0, 0, [0, 1, 2, 3])
-        prep_w(0, 1)
+        prep_w(0, 1, True)
         load_w(4, 0)
-        stage1(0, 0, [4, 5, 6])
+        stage1(0, 0, [[4, 5], [6]])
         prep_w(1, 0)
         load_w(4, 1)
-        stage1(0, 1, [0, 1, 2, 3])
-        prep_c(0, 4)
-        stage1(0, 1, [4, 5, 6])
         prep_w(1, 1)
-        stage1(1, 0, [0, 1, 2])
+        stage1(0, 1, pairs(7))
+        prep_c(0, 4)
         prep_c(4, 7)
-        stage1(1, 0, [3, 4, 5])
         prep_w(2, 0)
-        stage2(0)
-        stage1(1, 1, [0, 1, 2, 3, 4, 5])
         prep_w(2, 1)
-        stage2(1)
-        stage1(2, 0, [0, 1, 2, 3, 4])
-        prep_w(3, 0)
-        stage1(2, 1, [0, 1, 2, 3, 4])
-        prep_w(3, 1)
-        stage2(2)
-        stage1(3, 0, [0, 1, 2, 3])
-        prep_w(4, 0)
-        stage1(3, 1, [0, 1, 2, 3])
-        prep_w(4, 1)
-        stage2(3)
-        stage1(4, 0, [0, 1, 2])
-        stage1(4, 1, [0, 1, 2])
-        stage2(4)
+        stage1(1, 0, pairs(6), (), 2)
+        for k in range(2):
+            prep_w(k + 3, 0)
+            prep_w(k + 3, 1)
+            s2_matmuls(k)
+            urgent.extend([job_max_diag(k, b) for b in range(len(sc_banks[k]))])
+            stage1(k + 1, 1, pairs(N_SLICE - k - 1))
+            all_exps(k)
+            stage1(k + 2, 0, pairs(N_SLICE - k - 2))
+        s2_matmuls(2)
+        urgent.extend([job_max_diag(2, b) for b in range(len(sc_banks[2]))])
+        stage1(3, 1, pairs(4))
+        all_exps(2)
+        stage1(4, 0, [[0, 1]])
+        s2_matmuls(3, (0, 4), ring)
+        urgent.append(job_max_diag(3, 0))
+        stage1(4, 0, [[2]])
+        stage1(4, 1, pairs(3))
+        flush_jobs()
+        all_exps(3)
 
         n_col = B_LO * N_GROUP
+        n_early = B_LO * GROUP0[4]
+        s2_matmuls(4, (0, 2))
+        s2_max(4)
+        exps(4, 0)
+        exps(4, 1)
         nc.scalar.activation(out=warm[:, 1:2], in_=sumexp[:, N_GROUP - 1 : N_GROUP], func=ACT.Ln)
-        zd = ring.tile([P, 512], F32, name="zd", tag="bank")
-        nc.tensor.matmul(zd[:, 0:n_col], lhsT=fold[:], rhs=spread_d[:], start=True, stop=True)
+        flush_jobs()
         zs = ring.tile([P, 512], F32, name="zs", tag="bank")
-        nc.tensor.matmul(zs[:, 0:n_col], lhsT=fold[:], rhs=spread_s[:], start=True, stop=True)
+        zd = ring.tile([P, 512], F32, name="zd", tag="bank")
+        nc.tensor.matmul(zs[:, 0:n_early], lhsT=fold[:], rhs=spread_s[:, 0:n_early], start=True, stop=True)
+        nc.tensor.matmul(zd[:, 0:n_early], lhsT=fold[:], rhs=spread_d[:, 0:n_early], start=True, stop=True)
+        spread_sum(4)
+        nc.tensor.matmul(zs[:, n_early:n_col], lhsT=fold[:], rhs=spread_s[:, n_early:n_col], start=True, stop=True)
+        diag(4, 0)
+        diag(4, 1)
+        spread_diag(4)
+        nc.tensor.matmul(zd[:, n_early:n_col], lhsT=fold[:], rhs=spread_d[:, n_early:n_col], start=True, stop=True)
         lnz = keep.tile([P, n_col], F32, name="lnz")
         nc.scalar.activation(out=lnz[0:B_HI, :], in_=zs[0:B_HI, 0:n_col], func=ACT.Ln)
         res = keep.tile([P, n_col], F32, name="res")

@@ -23,7 +23,7 @@ B_HI = 16
 FLOPS = 2 * N_GROUP * P * FEAT * FEAT + 2 * N_GROUP * P * P * FEAT
 
 QW = 2
-HALF = (1, 4, 7)
+HALF = (0, 2, 4, 6)
 PINNED = True
 
 
@@ -149,7 +149,7 @@ def tile_infonceloss_pa_kernel(tc, embeddings, contexts, W, out):
                     nc.tensor.transpose(bank[:, j, :], words[:, P * j : P * (j + 1)], ident[:])
                 dst = grp[:, i, :].bitcast(F32).rearrange("p (g r u) -> p g r u", g=2, u=2)
                 src = bank[:].rearrange("p (g u) r -> p g r u", u=2)
-                if turn[0] % 8 in vector_share:
+                if i in vector_share:
                     nc.vector.tensor_copy(out=dst, in_=src)
                 else:
                     nc.scalar.copy(out=dst, in_=src)
@@ -166,14 +166,14 @@ def tile_infonceloss_pa_kernel(tc, embeddings, contexts, W, out):
         def job_quantise(codes, scales, values):
             return lambda: quantise(codes, scales, values)
 
-        def prep_x(t0, t1, now=True, share=HALF):
+        def prep_x(t0, t1, now=True, share=(0, 2)):
             prep([x_raw[:, t, :] for t in range(t0, t1)], xq[:, t0:t1, :], xs[:, t0:t1, :], now, share)
 
-        def prep_c(t0, t1, now=False, share=HALF):
+        def prep_c(t0, t1, now=False, share=(0, 2)):
             prep([c_raw[:, t, :] for t in range(t0, t1)], cq[:, t0:t1, :], cs[:, t0:t1, :], now, share)
             ready_at["c"] = len(backlog)
 
-        def prep_w(k, g, now=False, share=HALF):
+        def prep_w(k, g, now=False, share=(0, 2)):
             t = w_raw[(k, g)]
             prep([t[:, j, :] for j in range(4)], wq[k][:, 4 * g : 4 * g + 4, :], ws[k][:, 4 * g : 4 * g + 4, :], now, share)
             ready_at[(k, g)] = len(backlog)
@@ -330,28 +330,40 @@ def tile_infonceloss_pa_kernel(tc, embeddings, contexts, W, out):
         load_w(3, 1)
         prep_x(1, 2)
         prep_x(2, 4)
-        stage1(0, 0, pairs(4))
+        stage1(0, 0, [[0, 1]])
         prep_x(4, 7)
+        stage1(0, 0, [[2, 3]])
         prep_w(0, 1, True)
         load_w(4, 0)
         stage1(0, 0, [[4, 5], [6]])
         prep_w(1, 0)
         load_w(4, 1)
+        stage1(0, 1, [[0, 1], [2, 3]])
         prep_w(1, 1)
-        stage1(0, 1, pairs(7))
+        stage1(0, 1, [[4, 5], [6]])
         prep_c(0, 4)
+        stage1(1, 0, [[0, 1], [2, 3]])
         prep_c(4, 7)
+        stage1(1, 0, [[4, 5]])
         prep_w(2, 0)
+        s2_matmuls(0)
+        urgent.extend([job_max_diag(0, b) for b in range(2)])
+        stage1(1, 1, [[0, 1], [2, 3]])
         prep_w(2, 1)
-        stage1(1, 0, pairs(6), (), 2)
-        for k in range(2):
-            prep_w(k + 3, 0)
-            prep_w(k + 3, 1)
-            s2_matmuls(k)
-            urgent.extend([job_max_diag(k, b) for b in range(len(sc_banks[k]))])
-            stage1(k + 1, 1, pairs(N_SLICE - k - 1))
-            all_exps(k)
-            stage1(k + 2, 0, pairs(N_SLICE - k - 2))
+        stage1(1, 1, [[4, 5]])
+        all_exps(0)
+        prep_w(3, 0)
+        stage1(2, 0, [[0, 1], [2, 3]])
+        prep_w(3, 1)
+        stage1(2, 0, [[4]])
+        prep_w(4, 0)
+        s2_matmuls(1)
+        urgent.extend([job_max_diag(1, b) for b in range(2)])
+        stage1(2, 1, [[0, 1], [2, 3]])
+        prep_w(4, 1)
+        stage1(2, 1, [[4]])
+        all_exps(1)
+        stage1(3, 0, pairs(4))
         s2_matmuls(2)
         urgent.extend([job_max_diag(2, b) for b in range(len(sc_banks[2]))])
         stage1(3, 1, pairs(4))

@@ -16,15 +16,13 @@ P = 128
 FEAT = 1024
 N_STEP = 5
 N_SLICE = 7
+TILE_WORDS = FEAT // 4
 GROUP0 = [0, 7, 13, 18, 22]
 N_GROUP = 25
 B_LO = 8
-B_HI = 16
+B_HI = P // B_LO
+W_BUFFERS = 7
 FLOPS = 2 * N_GROUP * P * FEAT * FEAT + 2 * N_GROUP * P * P * FEAT
-
-QW = 2
-HALF = (0, 2, 4, 6)
-PINNED = True
 
 
 def tile_infonceloss_pa_kernel(tc, embeddings, contexts, W, out):
@@ -32,15 +30,14 @@ def tile_infonceloss_pa_kernel(tc, embeddings, contexts, W, out):
     with ExitStack() as ctx:
         const = ctx.enter_context(tc.tile_pool(name="const", bufs=1))
         raw = ctx.enter_context(tc.tile_pool(name="raw", bufs=1))
-        wraw_pool = ctx.enter_context(tc.tile_pool(name="wraw", bufs=7))
+        wraw_pool = ctx.enter_context(tc.tile_pool(name="wraw", bufs=W_BUFFERS))
         grp_pool = ctx.enter_context(tc.tile_pool(name="grp", bufs=4))
         keep = ctx.enter_context(tc.tile_pool(name="keep", bufs=1))
         xwg_pool = ctx.enter_context(tc.tile_pool(name="xwg", bufs=4))
         junk = ctx.enter_context(tc.tile_pool(name="junk", bufs=2))
         ring = ctx.enter_context(tc.psum_pool(name="ring", bufs=6))
         scp = ctx.enter_context(tc.psum_pool(name="scores", bufs=2))
-        if PINNED:
-            ctx.enter_context(tc.manual_schedule())
+        ctx.enter_context(tc.manual_schedule())
 
         x_raw = raw.tile([P, N_SLICE, FEAT], BF16, name="x_raw")
         c_raw = raw.tile([P, N_SLICE, FEAT], BF16, name="c_raw")
@@ -52,28 +49,29 @@ def tile_infonceloss_pa_kernel(tc, embeddings, contexts, W, out):
         def load_c(t0, t1):
             nc.sync.dma_start(out=c_raw[:, t0:t1, :], in_=contexts[:, t0:t1, :])
 
-        def load_w(k, g, pieces=1):
+        def load_w(half, pieces=1):
+            k, g = half // 2, half % 2
             t = wraw_pool.tile([P, 4, FEAT], BF16, name="w_raw", tag="w_raw")
-            dst = t[:].rearrange("p (u e) d -> p u (e d)", e=2)
-            src = W[k, 512 * g : 512 * (g + 1), :].rearrange("(u p e) d -> p u (e d)", u=2, e=2)
+            dst = t[:].rearrange("p (u i) d -> p u (i d)", i=2)
+            src = W[k, 512 * g : 512 * (g + 1), :].rearrange("(u p i) d -> p u (i d)", u=2, i=2)
             step = 2 // pieces
             for u in range(0, 2, step):
                 nc.sync.dma_start(out=dst[:, u : u + step, :], in_=src[:, u : u + step, :])
-            w_raw[(k, g)] = t
+            w_raw[half] = t
 
         load_x(0, 1)
-        load_w(0, 0, 2)
+        load_w(0, pieces=2)
         load_x(1, 2)
         load_x(2, 4)
         load_x(4, 7)
-        load_w(0, 1)
-        load_w(1, 0)
-        load_w(1, 1)
+        load_w(1)
+        load_w(2)
+        load_w(3)
         load_c(0, 4)
         load_c(4, 7)
-        load_w(2, 0)
-        load_w(2, 1)
-        load_w(3, 0)
+        load_w(4)
+        load_w(5)
+        load_w(6)
 
         ident = const.tile([P, P], F32, name="ident")
         make_identity(nc, ident[:])
@@ -90,12 +88,12 @@ def tile_infonceloss_pa_kernel(tc, embeddings, contexts, W, out):
             out=fold[:, 0:B_HI], in_=ident[:].rearrange("p (q l) -> p q l", l=B_LO), axis=AX.X, op=ALU.add
         )
 
-        xq = keep.tile([P, N_SLICE, 256], U32, name="xq", align_bytes=64)
-        xs = keep.tile([P, N_SLICE, 256], U8, name="xs", align_bytes=64)
-        cq = keep.tile([P, N_SLICE, 256], U32, name="cq", align_bytes=64)
-        cs = keep.tile([P, N_SLICE, 256], U8, name="cs", align_bytes=64)
-        wq = [keep.tile([P, 8, 256], U32, name="wq%d" % k, align_bytes=64) for k in range(N_STEP)]
-        ws = [keep.tile([P, 8, 256], U8, name="ws%d" % k, align_bytes=64) for k in range(N_STEP)]
+        xq = keep.tile([P, N_SLICE, TILE_WORDS], U32, name="xq", align_bytes=64)
+        xs = keep.tile([P, N_SLICE, TILE_WORDS], U8, name="xs", align_bytes=64)
+        cq = keep.tile([P, N_SLICE, TILE_WORDS], U32, name="cq", align_bytes=64)
+        cs = keep.tile([P, N_SLICE, TILE_WORDS], U8, name="cs", align_bytes=64)
+        wq = [keep.tile([P, 8, TILE_WORDS], U32, name="wq%d" % k, align_bytes=64) for k in range(N_STEP)]
+        ws = [keep.tile([P, 8, TILE_WORDS], U8, name="ws%d" % k, align_bytes=64) for k in range(N_STEP)]
         xwq = keep.tile([P, 2 * N_GROUP, P], U32, name="xwq", align_bytes=64)
         xws = keep.tile([P, 2 * N_GROUP, P], U8, name="xws", align_bytes=64)
         negmax = keep.tile([P, N_GROUP], F32, name="negmax")
@@ -104,171 +102,105 @@ def tile_infonceloss_pa_kernel(tc, embeddings, contexts, W, out):
         spread_s = keep.tile([P, B_LO * N_GROUP], F32, name="spread_s")
         spread_d = keep.tile([P, B_LO * N_GROUP], F32, name="spread_d")
 
-        urgent = []
-        urgent_done = [0]
-        backlog = []
-        backlog_done = [0]
-        ready_at = {}
-
-        def next_job():
-            if urgent_done[0] < len(urgent):
-                urgent[urgent_done[0]]()
-                urgent_done[0] += 1
-            elif backlog_done[0] < len(backlog):
-                backlog[backlog_done[0]]()
-                backlog_done[0] += 1
-
-        def need(key):
-            for i in range(backlog_done[0], ready_at.get(key, 0)):
-                backlog[i]()
-            backlog_done[0] = max(backlog_done[0], ready_at.get(key, 0))
-
-        def flush_jobs():
-            for i in range(urgent_done[0], len(urgent)):
-                urgent[i]()
-            urgent_done[0] = len(urgent)
-            for i in range(backlog_done[0], len(backlog)):
-                backlog[i]()
-            backlog_done[0] = len(backlog)
-
         def flat(ap):
             return ap.rearrange("p i c -> p (i c)")
 
         def quantise(codes, scales, values):
             nc.vector.quantize_mx(out=flat(codes).bitcast(FP8X4), scales=flat(scales), in_=flat(values))
 
-        turn = [0]
+        def quantise_tiles(grp, n, codes, scales, widest):
+            i0 = 0
+            for w in (4, 2, 1):
+                if w <= widest:
+                    for call in range((n - i0) // w):
+                        quantise(codes[:, i0 : i0 + w, :], scales[:, i0 : i0 + w, :], grp[:, i0 : i0 + w, :])
+                        i0 += w
 
-        def prep(rows, codes, scales, now, vector_share):
-            n = len(rows)
+        def transposes(rows):
             grp = grp_pool.tile([P, 4, FEAT], BF16, name="grp", tag="grp", align_bytes=64)
-            for i in range(n):
+            for i in range(len(rows)):
                 bank = ring.tile([P, 4, P], F32, name="bank", tag="bank")
                 words = rows[i].bitcast(F32)
                 for j in range(4):
                     nc.tensor.transpose(bank[:, j, :], words[:, P * j : P * (j + 1)], ident[:])
                 dst = grp[:, i, :].bitcast(F32).rearrange("p (g r u) -> p g r u", g=2, u=2)
                 src = bank[:].rearrange("p (g u) r -> p g r u", u=2)
-                if i in vector_share:
+                if i % 2 == 0:
                     nc.vector.tensor_copy(out=dst, in_=src)
                 else:
                     nc.scalar.copy(out=dst, in_=src)
-                turn[0] += 1
-            for i0 in range(0, n, QW):
-                w = min(QW, n - i0)
-                assert w in (1, 2, 4)
-                job = job_quantise(codes[:, i0 : i0 + w, :], scales[:, i0 : i0 + w, :], grp[:, i0 : i0 + w, :])
-                if now:
-                    job()
-                else:
-                    backlog.append(job)
+            return grp
 
-        def job_quantise(codes, scales, values):
-            return lambda: quantise(codes, scales, values)
-
-        def prep_x(t0, t1, now=True, share=(0, 2)):
-            prep([x_raw[:, t, :] for t in range(t0, t1)], xq[:, t0:t1, :], xs[:, t0:t1, :], now, share)
-
-        def prep_c(t0, t1, now=False, share=(0, 2)):
-            prep([c_raw[:, t, :] for t in range(t0, t1)], cq[:, t0:t1, :], cs[:, t0:t1, :], now, share)
-            ready_at["c"] = len(backlog)
-
-        def prep_w(k, g, now=False, share=(0, 2)):
-            t = w_raw[(k, g)]
-            prep([t[:, j, :] for j in range(4)], wq[k][:, 4 * g : 4 * g + 4, :], ws[k][:, 4 * g : 4 * g + 4, :], now, share)
-            ready_at[(k, g)] = len(backlog)
+        def operand(kind, a, b):
+            if kind == "x":
+                return [x_raw[:, t, :] for t in range(a, b)], xq[:, a:b, :], xs[:, a:b, :]
+            if kind == "c":
+                return [c_raw[:, t, :] for t in range(a, b)], cq[:, a:b, :], cs[:, a:b, :]
+            k, g = a // 2, a % 2
+            tiles = slice(4 * g, 4 * g + 4)
+            return [w_raw[a][:, j, :] for j in range(4)], wq[k][:, tiles, :], ws[k][:, tiles, :]
 
         def xw_row(k, g2, s):
             return 2 * GROUP0[k] + g2 * (N_SLICE - k) + s
 
-        def stage1(k, g2, chunks, vector_banks=(), per_slot=1):
-            need((k, g2))
-            for i in range(per_slot):
-                next_job()
-            for chunk in chunks:
-                n = len(chunk)
-                xwg = xwg_pool.tile([P, 2, 512], BF16, name="xwg", tag="xwg", align_bytes=64)
-                for i in range(n):
-                    s = chunk[i]
-                    bank = ring.tile([P, 4, P], F32, name="bank", tag="bank")
-                    for t in range(4):
-                        for g1 in range(2):
-                            cols = slice(P * g1, P * (g1 + 1))
-                            nc.tensor.matmul_mx(
-                                out=bank[:, t, :],
-                                lhsT=wq[k][:, 4 * g2 + t, cols].bitcast(FP8X4),
-                                lhsT_scale=ws[k][:, 4 * g2 + t, cols],
-                                rhs=xq[:, k + s, cols].bitcast(FP8X4),
-                                rhs_scale=xs[:, k + s, cols],
-                                start=(g1 == 0),
-                                stop=(g1 == 1),
-                            )
-                    dst = xwg[:, i, :].rearrange("p (b t) -> p b t", t=4)
-                    src = bank[:].rearrange("p t b -> p b t")
-                    if s in vector_banks:
-                        nc.vector.tensor_copy(out=dst, in_=src)
-                    else:
-                        nc.scalar.copy(out=dst, in_=src)
-                r0 = xw_row(k, g2, chunk[0])
-                quantise(xwq[:, r0 : r0 + n, :], xws[:, r0 : r0 + n, :], xwg[:, 0:n, :])
-                for i in range(per_slot):
-                    next_job()
+        def stage1(k, g2, slices):
+            xwg = xwg_pool.tile([P, 2, 512], BF16, name="xwg", tag="xwg", align_bytes=64)
+            for i in range(len(slices)):
+                s = slices[i]
+                bank = ring.tile([P, 4, P], F32, name="bank", tag="bank")
+                for t in range(4):
+                    for g1 in range(2):
+                        cols = slice(P * g1, P * (g1 + 1))
+                        nc.tensor.matmul_mx(
+                            out=bank[:, t, :],
+                            lhsT=wq[k][:, 4 * g2 + t, cols].bitcast(FP8X4),
+                            lhsT_scale=ws[k][:, 4 * g2 + t, cols],
+                            rhs=xq[:, k + s, cols].bitcast(FP8X4),
+                            rhs_scale=xs[:, k + s, cols],
+                            start=(g1 == 0),
+                            stop=(g1 == 1),
+                        )
+                nc.scalar.copy(
+                    out=xwg[:, i, :].rearrange("p (b t) -> p b t", t=4),
+                    in_=bank[:].rearrange("p t b -> p b t"),
+                )
+            return xwg
 
-        def pairs(n):
-            return [list(range(s, min(s + 2, n))) for s in range(0, n, 2)]
+        def quantise_xw(k, g2, slices, xwg):
+            n = len(slices)
+            r0 = xw_row(k, g2, slices[0])
+            quantise(xwq[:, r0 : r0 + n, :], xws[:, r0 : r0 + n, :], xwg[:, 0:n, :])
 
-        sc_banks = {}
+        score_banks = {}
 
-        def s2_matmuls(k, s0_list=(0, 4), pool=None):
-            need("c")
+        def scores(k, first_slices):
             n_s = N_SLICE - k
-            sc_banks[k] = []
-            for j in range(len(s0_list)):
-                s0 = s0_list[j]
-                if s0 >= n_s:
-                    continue
-                n = min(s0_list[j + 1] if j + 1 < len(s0_list) else n_s, n_s) - s0
-                if pool is None:
-                    sc = scp.tile([P, 4, P], F32, name="sc", tag="sc")
-                else:
-                    sc = pool.tile([P, 4, P], F32, name="bank", tag="bank")
+            score_banks[k] = []
+            for j in range(len(first_slices)):
+                s0 = first_slices[j]
+                n = (first_slices[j + 1] if j + 1 < len(first_slices) else n_s) - s0
+                sc = scp.tile([P, 4, P], F32, name="sc", tag="sc")
                 for i in range(n):
-                    s = s0 + i
                     for g2 in range(2):
-                        r = xw_row(k, g2, s)
+                        r = xw_row(k, g2, s0 + i)
                         cols = slice(P * g2, P * (g2 + 1))
                         nc.tensor.matmul_mx(
                             out=sc[:, i, :],
                             lhsT=xwq[:, r, :].bitcast(FP8X4),
                             lhsT_scale=xws[:, r, :],
-                            rhs=cq[:, s, cols].bitcast(FP8X4),
-                            rhs_scale=cs[:, s, cols],
+                            rhs=cq[:, s0 + i, cols].bitcast(FP8X4),
+                            rhs_scale=cs[:, s0 + i, cols],
                             start=(g2 == 0),
                             stop=(g2 == 1),
                         )
-                sc_banks[k].append((sc, GROUP0[k] + s0, n))
+                score_banks[k].append((sc, GROUP0[k] + s0, n))
 
-        def s2_max(k):
-            for sc, gi, n in sc_banks[k]:
-                nc.vector.tensor_reduce(
-                    out=negmax[:, gi : gi + n], in_=sc[:, 0:n, :], axis=AX.X, op=ALU.max, negate=True
-                )
+        def row_max(k, b):
+            sc, gi, n = score_banks[k][b]
+            nc.vector.tensor_reduce(out=negmax[:, gi : gi + n], in_=sc[:, 0:n, :], axis=AX.X, op=ALU.max, negate=True)
 
-        def exps(k, b):
-            sc, gi, n = sc_banks[k][b]
-            for i in range(n):
-                js = junk.tile([P, P], F32, name="js", tag="js")
-                nc.scalar.activation(
-                    out=js[:],
-                    in_=sc[:, i, :],
-                    func=ACT.Exp,
-                    bias=negmax[:, gi + i : gi + i + 1],
-                    scale=1.0,
-                    accum_out=sumexp[:, gi + i : gi + i + 1],
-                )
-
-        def diag(k, b):
-            sc, gi, n = sc_banks[k][b]
+        def diagonal(k, b):
+            sc, gi, n = score_banks[k][b]
             for i in range(n):
                 jv = junk.tile([P, P], F32, name="jv", tag="jv")
                 nc.vector.scalar_tensor_tensor(
@@ -281,118 +213,121 @@ def tile_infonceloss_pa_kernel(tc, embeddings, contexts, W, out):
                     accum_out=dm[:, gi + i : gi + i + 1],
                 )
 
-        def spread_diag(k):
-            n_s = N_SLICE - k
+        def exponentials(k, b):
+            sc, gi, n = score_banks[k][b]
+            for i in range(n):
+                js = junk.tile([P, P], F32, name="js", tag="js")
+                nc.scalar.activation(
+                    out=js[:],
+                    in_=sc[:, i, :],
+                    func=ACT.Exp,
+                    bias=negmax[:, gi + i : gi + i + 1],
+                    scale=1.0,
+                    accum_out=sumexp[:, gi + i : gi + i + 1],
+                )
+
+        def step_columns(tile, k):
             g0 = GROUP0[k]
+            return tile[:, B_LO * g0 : B_LO * (g0 + N_SLICE - k)].rearrange("p (l s) -> p l s", l=B_LO)
+
+        def spread_diagonal(k):
+            n_s = N_SLICE - k
             shape = [P, B_LO, n_s]
             nc.vector.tensor_tensor(
-                out=spread_d[:, B_LO * g0 : B_LO * (g0 + n_s)].rearrange("p (l s) -> p l s", l=B_LO),
-                in0=dm[:, g0 : g0 + n_s].unsqueeze(1).to_broadcast(shape),
+                out=step_columns(spread_d, k),
+                in0=dm[:, GROUP0[k] : GROUP0[k] + n_s].unsqueeze(1).to_broadcast(shape),
                 in1=mask8[:].unsqueeze(2).to_broadcast(shape),
                 op=ALU.mult,
             )
 
         def spread_sum(k):
             n_s = N_SLICE - k
-            g0 = GROUP0[k]
             shape = [P, B_LO, n_s]
             nc.vector.scalar_tensor_tensor(
-                out=spread_s[:, B_LO * g0 : B_LO * (g0 + n_s)].rearrange("p (l s) -> p l s", l=B_LO),
-                in0=sumexp[:, g0 : g0 + n_s].unsqueeze(1).to_broadcast(shape),
+                out=step_columns(spread_s, k),
+                in0=sumexp[:, GROUP0[k] : GROUP0[k] + n_s].unsqueeze(1).to_broadcast(shape),
                 scalar=1.0 / (P * n_s),
                 in1=mask8[:].unsqueeze(2).to_broadcast(shape),
                 op0=ALU.mult,
                 op1=ALU.mult,
             )
 
-        def job_max_diag(k, b):
-            def job():
-                sc, gi, n = sc_banks[k][b]
-                nc.vector.tensor_reduce(
-                    out=negmax[:, gi : gi + n], in_=sc[:, 0:n, :], axis=AX.X, op=ALU.max, negate=True
-                )
-                diag(k, b)
-            return job
+        chunks = []
+        last_chunk = []
+        for k in range(N_STEP):
+            for g2 in range(2):
+                for s in range(0, N_SLICE - k, 2):
+                    chunks.append((k, g2, list(range(s, min(s + 2, N_SLICE - k)))))
+            last_chunk.append(len(chunks) - 1)
+        groups = [[("x", 0, 1), ("w", 0, 0), ("x", 1, 2), ("x", 2, 4)], [("x", 4, 7)], [("w", 1, 0)], [("w", 2, 0)]]
+        groups += [[("w", 3, 0)], [("c", 0, 4)], [("c", 4, 7)]] + [[("w", half, 0)] for half in range(4, 2 * N_STEP)]
+        contexts_ready = 12
+        scores_before = [max(last_chunk[k] + 3, contexts_ready) for k in range(N_STEP - 1)]
+        n_groups = 0
+        unquantised = None
+        step = -1
+        since = 0
+        for j in range(len(chunks)):
+            staged = []
+            if n_groups < len(groups) and (j < 2 or j % 2 == 0):
+                for kind, a, b in groups[n_groups]:
+                    rows, codes, scales = operand(kind, a, b)
+                    grp = transposes(rows)
+                    if j == 0:
+                        quantise_tiles(grp, len(rows), codes, scales, 2)
+                    else:
+                        staged.append((grp, len(rows), codes, scales))
+                    if kind == "w" and a + W_BUFFERS < 2 * N_STEP:
+                        load_w(a + W_BUFFERS)
+                n_groups += 1
+            if unquantised is not None:
+                quantise_xw(unquantised[0], unquantised[1], unquantised[2], unquantised[3])
+            for grp, n, codes, scales in staged:
+                quantise_tiles(grp, n, codes, scales, 4)
+            since += 1
+            if j in scores_before:
+                step += 1
+                since = 0
+                scores(step, (0, 4) if N_SLICE - step > 4 else (0,))
+            k, g2, slices = chunks[j]
+            unquantised = (k, g2, slices, stage1(k, g2, slices))
+            if step >= 0:
+                two_banks = len(score_banks[step]) > 1
+                if since == 0:
+                    row_max(step, 0)
+                    diagonal(step, 0)
+                if since == 1:
+                    exponentials(step, 0)
+                    if two_banks:
+                        row_max(step, 1)
+                        diagonal(step, 1)
+                if since == 2 and two_banks:
+                    exponentials(step, 1)
+                if since == 3:
+                    spread_diagonal(step)
+                    spread_sum(step)
+        quantise_xw(unquantised[0], unquantised[1], unquantised[2], unquantised[3])
 
-        def job_spread(k):
-            def job():
-                spread_diag(k)
-                spread_sum(k)
-            return job
-
-        def all_exps(k):
-            for b in range(len(sc_banks[k])):
-                exps(k, b)
-            backlog.append(job_spread(k))
-
-        prep_x(0, 1)
-        prep_w(0, 0, True)
-        load_w(3, 1)
-        prep_x(1, 2)
-        prep_x(2, 4)
-        stage1(0, 0, [[0, 1]])
-        prep_x(4, 7)
-        stage1(0, 0, [[2, 3]])
-        prep_w(0, 1, True)
-        load_w(4, 0)
-        stage1(0, 0, [[4, 5], [6]])
-        prep_w(1, 0)
-        load_w(4, 1)
-        stage1(0, 1, [[0, 1], [2, 3]])
-        prep_w(1, 1)
-        stage1(0, 1, [[4, 5], [6]])
-        prep_c(0, 4)
-        stage1(1, 0, [[0, 1], [2, 3]])
-        prep_c(4, 7)
-        stage1(1, 0, [[4, 5]])
-        prep_w(2, 0)
-        s2_matmuls(0)
-        urgent.extend([job_max_diag(0, b) for b in range(2)])
-        stage1(1, 1, [[0, 1], [2, 3]])
-        prep_w(2, 1)
-        stage1(1, 1, [[4, 5]])
-        all_exps(0)
-        prep_w(3, 0)
-        stage1(2, 0, [[0, 1], [2, 3]])
-        prep_w(3, 1)
-        stage1(2, 0, [[4]])
-        prep_w(4, 0)
-        s2_matmuls(1)
-        urgent.extend([job_max_diag(1, b) for b in range(2)])
-        stage1(2, 1, [[0, 1], [2, 3]])
-        prep_w(4, 1)
-        stage1(2, 1, [[4]])
-        all_exps(1)
-        stage1(3, 0, pairs(4))
-        s2_matmuls(2)
-        urgent.extend([job_max_diag(2, b) for b in range(len(sc_banks[2]))])
-        stage1(3, 1, pairs(4))
-        all_exps(2)
-        stage1(4, 0, [[0, 1]])
-        s2_matmuls(3, (0, 4), ring)
-        urgent.append(job_max_diag(3, 0))
-        stage1(4, 0, [[2]])
-        stage1(4, 1, pairs(3))
-        flush_jobs()
-        all_exps(3)
-
+        last = N_STEP - 1
         n_col = B_LO * N_GROUP
-        n_early = B_LO * GROUP0[4]
-        s2_matmuls(4, (0, 2))
-        s2_max(4)
-        exps(4, 0)
-        exps(4, 1)
+        n_early = B_LO * GROUP0[last]
+        scores(last, (0, 2))
+        row_max(last, 0)
+        row_max(last, 1)
+        exponentials(last, 0)
+        exponentials(last, 1)
         nc.scalar.activation(out=warm[:, 1:2], in_=sumexp[:, N_GROUP - 1 : N_GROUP], func=ACT.Ln)
-        flush_jobs()
+        spread_diagonal(last - 1)
+        spread_sum(last - 1)
         zs = ring.tile([P, 512], F32, name="zs", tag="bank")
         zd = ring.tile([P, 512], F32, name="zd", tag="bank")
         nc.tensor.matmul(zs[:, 0:n_early], lhsT=fold[:], rhs=spread_s[:, 0:n_early], start=True, stop=True)
         nc.tensor.matmul(zd[:, 0:n_early], lhsT=fold[:], rhs=spread_d[:, 0:n_early], start=True, stop=True)
-        spread_sum(4)
+        spread_sum(last)
         nc.tensor.matmul(zs[:, n_early:n_col], lhsT=fold[:], rhs=spread_s[:, n_early:n_col], start=True, stop=True)
-        diag(4, 0)
-        diag(4, 1)
-        spread_diag(4)
+        diagonal(last, 0)
+        diagonal(last, 1)
+        spread_diagonal(last)
         nc.tensor.matmul(zd[:, n_early:n_col], lhsT=fold[:], rhs=spread_d[:, n_early:n_col], start=True, stop=True)
         lnz = keep.tile([P, n_col], F32, name="lnz")
         nc.scalar.activation(out=lnz[0:B_HI, :], in_=zs[0:B_HI, 0:n_col], func=ACT.Ln)
@@ -401,7 +336,8 @@ def tile_infonceloss_pa_kernel(tc, embeddings, contexts, W, out):
         for k in range(N_STEP):
             n_s = N_SLICE - k
             g0 = GROUP0[k]
-            nc.sync.dma_start(
+            queue = nc.sync if k % 2 == 0 else nc.scalar
+            queue.dma_start(
                 out=out[P * g0 : P * (g0 + n_s)].rearrange("(q c) -> q c", q=B_HI),
                 in_=res[0:B_HI, B_LO * g0 : B_LO * (g0 + n_s)],
             )

@@ -88,6 +88,16 @@ def tile_infonceloss_pa_kernel(tc, embeddings, contexts, W, out):
             out=fold[:, 0:B_HI], in_=ident[:].rearrange("p (q l) -> p q l", l=B_LO), axis=AX.X, op=ALU.add
         )
 
+        zeros = const.tile([P, 512], BF16, name="zeros")
+        nc.vector.memset(zeros[:], 0.0)
+        idle = scp.tile([P, 512], F32, name="idle", tag="sc")
+
+        def keep_busy(n_col):
+            nc.tensor.matmul(idle[:, 0:n_col], lhsT=zeros[:, 0:P], rhs=zeros[:, 0:n_col], start=True, stop=True)
+
+        for i in range(8):
+            keep_busy(512)
+
         xq = keep.tile([P, N_SLICE, TILE_WORDS], U32, name="xq", align_bytes=64)
         xs = keep.tile([P, N_SLICE, TILE_WORDS], U8, name="xs", align_bytes=64)
         cq = keep.tile([P, N_SLICE, TILE_WORDS], U32, name="cq", align_bytes=64)
@@ -116,13 +126,15 @@ def tile_infonceloss_pa_kernel(tc, embeddings, contexts, W, out):
                         quantise(codes[:, i0 : i0 + w, :], scales[:, i0 : i0 + w, :], grp[:, i0 : i0 + w, :])
                         i0 += w
 
-        def transposes(rows):
+        def transposes(rows, busy=False):
             grp = grp_pool.tile([P, 4, FEAT], BF16, name="grp", tag="grp", align_bytes=64)
             for i in range(len(rows)):
                 bank = ring.tile([P, 4, P], F32, name="bank", tag="bank")
                 words = rows[i].bitcast(F32)
                 for j in range(4):
                     nc.tensor.transpose(bank[:, j, :], words[:, P * j : P * (j + 1)], ident[:])
+                if busy:
+                    keep_busy(256)
                 dst = grp[:, i, :].bitcast(F32).rearrange("p (g r u) -> p g r u", g=2, u=2)
                 src = bank[:].rearrange("p (g u) r -> p g r u", u=2)
                 if i % 2 == 0:
@@ -272,7 +284,7 @@ def tile_infonceloss_pa_kernel(tc, embeddings, contexts, W, out):
             if n_groups < len(groups) and (j < 2 or j % 2 == 0):
                 for kind, a, b in groups[n_groups]:
                     rows, codes, scales = operand(kind, a, b)
-                    grp = transposes(rows)
+                    grp = transposes(rows, j == 0)
                     if j == 0:
                         quantise_tiles(grp, len(rows), codes, scales, 2)
                     else:

from contextlib import ExitStack

import concourse.mybir as mybir
from concourse.masks import make_identity

F32 = mybir.dt.float32
BF16 = mybir.dt.bfloat16
U32 = mybir.dt.uint32
U8 = mybir.dt.uint8
FP8X4 = mybir.dt.float8_e4m3fn_x4
ALU = mybir.AluOpType
ACT = mybir.ActivationFunctionType
AX = mybir.AxisListType

P = 128
FEAT = 1024
N_STEP = 5
N_SLICE = 7
TILE_WORDS = FEAT // 4
GROUP0 = [0, 7, 13, 18, 22]
N_GROUP = 25
B_LO = 8
B_HI = P // B_LO
W_BUFFERS = 7
FLOPS = 2 * N_GROUP * P * FEAT * FEAT + 2 * N_GROUP * P * P * FEAT


def tile_infonceloss_pa_kernel(tc, embeddings, contexts, W, out):
    nc = tc.nc
    with ExitStack() as ctx:
        const = ctx.enter_context(tc.tile_pool(name="const", bufs=1))
        raw = ctx.enter_context(tc.tile_pool(name="raw", bufs=1))
        wraw_pool = ctx.enter_context(tc.tile_pool(name="wraw", bufs=W_BUFFERS))
        grp_pool = ctx.enter_context(tc.tile_pool(name="grp", bufs=4))
        keep = ctx.enter_context(tc.tile_pool(name="keep", bufs=1))
        xwg_pool = ctx.enter_context(tc.tile_pool(name="xwg", bufs=4))
        junk = ctx.enter_context(tc.tile_pool(name="junk", bufs=2))
        ring = ctx.enter_context(tc.psum_pool(name="ring", bufs=6))
        scp = ctx.enter_context(tc.psum_pool(name="scores", bufs=2))
        ctx.enter_context(tc.manual_schedule())

        x_raw = raw.tile([P, N_SLICE, FEAT], BF16, name="x_raw")
        c_raw = raw.tile([P, N_SLICE, FEAT], BF16, name="c_raw")
        w_raw = {}

        def load_x(t0, t1):
            nc.sync.dma_start(out=x_raw[:, t0:t1, :], in_=embeddings[:, 1 + t0 : 1 + t1, :])

        def load_c(t0, t1):
            nc.sync.dma_start(out=c_raw[:, t0:t1, :], in_=contexts[:, t0:t1, :])

        def load_w(half, pieces=1):
            k, g = half // 2, half % 2
            t = wraw_pool.tile([P, 4, FEAT], BF16, name="w_raw", tag="w_raw")
            dst = t[:].rearrange("p (u i) d -> p u (i d)", i=2)
            src = W[k, 512 * g : 512 * (g + 1), :].rearrange("(u p i) d -> p u (i d)", u=2, i=2)
            step = 2 // pieces
            for u in range(0, 2, step):
                nc.sync.dma_start(out=dst[:, u : u + step, :], in_=src[:, u : u + step, :])
            w_raw[half] = t

        load_x(0, 1)
        load_w(0, pieces=2)
        load_x(1, 2)
        load_x(2, 4)
        load_x(4, 7)
        load_w(1)
        load_w(2)
        load_w(3)
        load_c(0, 4)
        load_c(4, 7)
        load_w(4)
        load_w(5)
        load_w(6)

        ident = const.tile([P, P], F32, name="ident")
        make_identity(nc, ident[:])
        warm = const.tile([P, 2], F32, name="warm")
        nc.vector.memset(warm[:], 1.0)
        nc.scalar.activation(out=warm[:, 1:2], in_=warm[:, 0:1], func=ACT.Exp)
        mask8 = const.tile([P, B_LO], F32, name="mask8")
        nc.vector.tensor_reduce(
            out=mask8[:], in_=ident[:].rearrange("p (q l) -> p l q", l=B_LO), axis=AX.X, op=ALU.add
        )
        fold = const.tile([P, P], F32, name="fold")
        nc.vector.memset(fold[:], 0.0)
        nc.vector.tensor_reduce(
            out=fold[:, 0:B_HI], in_=ident[:].rearrange("p (q l) -> p q l", l=B_LO), axis=AX.X, op=ALU.add
        )

        zeros = const.tile([P, 512], BF16, name="zeros")
        nc.vector.memset(zeros[:], 0.0)
        idle = scp.tile([P, 512], F32, name="idle", tag="sc")

        def keep_busy(n_col):
            nc.tensor.matmul(idle[:, 0:n_col], lhsT=zeros[:, 0:P], rhs=zeros[:, 0:n_col], start=True, stop=True)

        for i in range(8):
            keep_busy(512)

        xq = keep.tile([P, N_SLICE, TILE_WORDS], U32, name="xq", align_bytes=64)
        xs = keep.tile([P, N_SLICE, TILE_WORDS], U8, name="xs", align_bytes=64)
        cq = keep.tile([P, N_SLICE, TILE_WORDS], U32, name="cq", align_bytes=64)
        cs = keep.tile([P, N_SLICE, TILE_WORDS], U8, name="cs", align_bytes=64)
        wq = [keep.tile([P, 8, TILE_WORDS], U32, name="wq%d" % k, align_bytes=64) for k in range(N_STEP)]
        ws = [keep.tile([P, 8, TILE_WORDS], U8, name="ws%d" % k, align_bytes=64) for k in range(N_STEP)]
        xwq = keep.tile([P, 2 * N_GROUP, P], U32, name="xwq", align_bytes=64)
        xws = keep.tile([P, 2 * N_GROUP, P], U8, name="xws", align_bytes=64)
        negmax = keep.tile([P, N_GROUP], F32, name="negmax")
        sumexp = keep.tile([P, N_GROUP], F32, name="sumexp")
        dm = keep.tile([P, N_GROUP], F32, name="dm")
        spread_s = keep.tile([P, B_LO * N_GROUP], F32, name="spread_s")
        spread_d = keep.tile([P, B_LO * N_GROUP], F32, name="spread_d")

        def flat(ap):
            return ap.rearrange("p i c -> p (i c)")

        def quantise(codes, scales, values):
            nc.vector.quantize_mx(out=flat(codes).bitcast(FP8X4), scales=flat(scales), in_=flat(values))

        def quantise_tiles(grp, n, codes, scales, widest):
            i0 = 0
            for w in (4, 2, 1):
                if w <= widest:
                    for call in range((n - i0) // w):
                        quantise(codes[:, i0 : i0 + w, :], scales[:, i0 : i0 + w, :], grp[:, i0 : i0 + w, :])
                        i0 += w

        def transposes(rows, busy=False):
            grp = grp_pool.tile([P, 4, FEAT], BF16, name="grp", tag="grp", align_bytes=64)
            for i in range(len(rows)):
                bank = ring.tile([P, 4, P], F32, name="bank", tag="bank")
                words = rows[i].bitcast(F32)
                for j in range(4):
                    nc.tensor.transpose(bank[:, j, :], words[:, P * j : P * (j + 1)], ident[:])
                if busy:
                    keep_busy(256)
                dst = grp[:, i, :].bitcast(F32).rearrange("p (g r u) -> p g r u", g=2, u=2)
                src = bank[:].rearrange("p (g u) r -> p g r u", u=2)
                if i % 2 == 0:
                    nc.vector.tensor_copy(out=dst, in_=src)
                else:
                    nc.scalar.copy(out=dst, in_=src)
            return grp

        def operand(kind, a, b):
            if kind == "x":
                return [x_raw[:, t, :] for t in range(a, b)], xq[:, a:b, :], xs[:, a:b, :]
            if kind == "c":
                return [c_raw[:, t, :] for t in range(a, b)], cq[:, a:b, :], cs[:, a:b, :]
            k, g = a // 2, a % 2
            tiles = slice(4 * g, 4 * g + 4)
            return [w_raw[a][:, j, :] for j in range(4)], wq[k][:, tiles, :], ws[k][:, tiles, :]

        def xw_row(k, g2, s):
            return 2 * GROUP0[k] + g2 * (N_SLICE - k) + s

        def stage1(k, g2, slices):
            xwg = xwg_pool.tile([P, 2, 512], BF16, name="xwg", tag="xwg", align_bytes=64)
            for i in range(len(slices)):
                s = slices[i]
                bank = ring.tile([P, 4, P], F32, name="bank", tag="bank")
                for t in range(4):
                    for g1 in range(2):
                        cols = slice(P * g1, P * (g1 + 1))
                        nc.tensor.matmul_mx(
                            out=bank[:, t, :],
                            lhsT=wq[k][:, 4 * g2 + t, cols].bitcast(FP8X4),
                            lhsT_scale=ws[k][:, 4 * g2 + t, cols],
                            rhs=xq[:, k + s, cols].bitcast(FP8X4),
                            rhs_scale=xs[:, k + s, cols],
                            start=(g1 == 0),
                            stop=(g1 == 1),
                        )
                nc.scalar.copy(
                    out=xwg[:, i, :].rearrange("p (b t) -> p b t", t=4),
                    in_=bank[:].rearrange("p t b -> p b t"),
                )
            return xwg

        def quantise_xw(k, g2, slices, xwg):
            n = len(slices)
            r0 = xw_row(k, g2, slices[0])
            quantise(xwq[:, r0 : r0 + n, :], xws[:, r0 : r0 + n, :], xwg[:, 0:n, :])

        score_banks = {}

        def scores(k, first_slices):
            n_s = N_SLICE - k
            score_banks[k] = []
            for j in range(len(first_slices)):
                s0 = first_slices[j]
                n = (first_slices[j + 1] if j + 1 < len(first_slices) else n_s) - s0
                sc = scp.tile([P, 4, P], F32, name="sc", tag="sc")
                for i in range(n):
                    for g2 in range(2):
                        r = xw_row(k, g2, s0 + i)
                        cols = slice(P * g2, P * (g2 + 1))
                        nc.tensor.matmul_mx(
                            out=sc[:, i, :],
                            lhsT=xwq[:, r, :].bitcast(FP8X4),
                            lhsT_scale=xws[:, r, :],
                            rhs=cq[:, s0 + i, cols].bitcast(FP8X4),
                            rhs_scale=cs[:, s0 + i, cols],
                            start=(g2 == 0),
                            stop=(g2 == 1),
                        )
                score_banks[k].append((sc, GROUP0[k] + s0, n))

        def row_max(k, b):
            sc, gi, n = score_banks[k][b]
            nc.vector.tensor_reduce(out=negmax[:, gi : gi + n], in_=sc[:, 0:n, :], axis=AX.X, op=ALU.max, negate=True)

        def diagonal(k, b):
            sc, gi, n = score_banks[k][b]
            for i in range(n):
                jv = junk.tile([P, P], F32, name="jv", tag="jv")
                nc.vector.scalar_tensor_tensor(
                    out=jv[:],
                    in0=sc[:, i, :],
                    scalar=negmax[:, gi + i : gi + i + 1],
                    in1=ident[:],
                    op0=ALU.add,
                    op1=ALU.mult,
                    accum_out=dm[:, gi + i : gi + i + 1],
                )

        def exponentials(k, b):
            sc, gi, n = score_banks[k][b]
            for i in range(n):
                js = junk.tile([P, P], F32, name="js", tag="js")
                nc.scalar.activation(
                    out=js[:],
                    in_=sc[:, i, :],
                    func=ACT.Exp,
                    bias=negmax[:, gi + i : gi + i + 1],
                    scale=1.0,
                    accum_out=sumexp[:, gi + i : gi + i + 1],
                )

        def step_columns(tile, k):
            g0 = GROUP0[k]
            return tile[:, B_LO * g0 : B_LO * (g0 + N_SLICE - k)].rearrange("p (l s) -> p l s", l=B_LO)

        def spread_diagonal(k):
            n_s = N_SLICE - k
            shape = [P, B_LO, n_s]
            nc.vector.tensor_tensor(
                out=step_columns(spread_d, k),
                in0=dm[:, GROUP0[k] : GROUP0[k] + n_s].unsqueeze(1).to_broadcast(shape),
                in1=mask8[:].unsqueeze(2).to_broadcast(shape),
                op=ALU.mult,
            )

        def spread_sum(k):
            n_s = N_SLICE - k
            shape = [P, B_LO, n_s]
            nc.vector.scalar_tensor_tensor(
                out=step_columns(spread_s, k),
                in0=sumexp[:, GROUP0[k] : GROUP0[k] + n_s].unsqueeze(1).to_broadcast(shape),
                scalar=1.0 / (P * n_s),
                in1=mask8[:].unsqueeze(2).to_broadcast(shape),
                op0=ALU.mult,
                op1=ALU.mult,
            )

        chunks = []
        last_chunk = []
        for k in range(N_STEP):
            for g2 in range(2):
                for s in range(0, N_SLICE - k, 2):
                    chunks.append((k, g2, list(range(s, min(s + 2, N_SLICE - k)))))
            last_chunk.append(len(chunks) - 1)
        groups = [[("x", 0, 1), ("w", 0, 0), ("x", 1, 2), ("x", 2, 4)], [("x", 4, 7)], [("w", 1, 0)], [("w", 2, 0)]]
        groups += [[("w", 3, 0)], [("c", 0, 4)], [("c", 4, 7)]] + [[("w", half, 0)] for half in range(4, 2 * N_STEP)]
        contexts_ready = 12
        scores_before = [max(last_chunk[k] + 3, contexts_ready) for k in range(N_STEP - 1)]
        n_groups = 0
        unquantised = None
        step = -1
        since = 0
        for j in range(len(chunks)):
            staged = []
            if n_groups < len(groups) and (j < 2 or j % 2 == 0):
                for kind, a, b in groups[n_groups]:
                    rows, codes, scales = operand(kind, a, b)
                    grp = transposes(rows, j == 0)
                    if j == 0:
                        quantise_tiles(grp, len(rows), codes, scales, 2)
                    else:
                        staged.append((grp, len(rows), codes, scales))
                    if kind == "w" and a + W_BUFFERS < 2 * N_STEP:
                        load_w(a + W_BUFFERS)
                n_groups += 1
            if unquantised is not None:
                quantise_xw(unquantised[0], unquantised[1], unquantised[2], unquantised[3])
            for grp, n, codes, scales in staged:
                quantise_tiles(grp, n, codes, scales, 4)
            since += 1
            if j in scores_before:
                step += 1
                since = 0
                scores(step, (0, 4) if N_SLICE - step > 4 else (0,))
            k, g2, slices = chunks[j]
            unquantised = (k, g2, slices, stage1(k, g2, slices))
            if step >= 0:
                two_banks = len(score_banks[step]) > 1
                if since == 0:
                    row_max(step, 0)
                    diagonal(step, 0)
                if since == 1:
                    exponentials(step, 0)
                    if two_banks:
                        row_max(step, 1)
                        diagonal(step, 1)
                if since == 2 and two_banks:
                    exponentials(step, 1)
                if since == 3:
                    spread_diagonal(step)
                    spread_sum(step)
        quantise_xw(unquantised[0], unquantised[1], unquantised[2], unquantised[3])

        last = N_STEP - 1
        n_col = B_LO * N_GROUP
        n_early = B_LO * GROUP0[last]
        scores(last, (0, 2))
        row_max(last, 0)
        row_max(last, 1)
        exponentials(last, 0)
        exponentials(last, 1)
        nc.scalar.activation(out=warm[:, 1:2], in_=sumexp[:, N_GROUP - 1 : N_GROUP], func=ACT.Ln)
        spread_diagonal(last - 1)
        spread_sum(last - 1)
        zs = ring.tile([P, 512], F32, name="zs", tag="bank")
        zd = ring.tile([P, 512], F32, name="zd", tag="bank")
        nc.tensor.matmul(zs[:, 0:n_early], lhsT=fold[:], rhs=spread_s[:, 0:n_early], start=True, stop=True)
        nc.tensor.matmul(zd[:, 0:n_early], lhsT=fold[:], rhs=spread_d[:, 0:n_early], start=True, stop=True)
        spread_sum(last)
        nc.tensor.matmul(zs[:, n_early:n_col], lhsT=fold[:], rhs=spread_s[:, n_early:n_col], start=True, stop=True)
        diagonal(last, 0)
        diagonal(last, 1)
        spread_diagonal(last)
        nc.tensor.matmul(zd[:, n_early:n_col], lhsT=fold[:], rhs=spread_d[:, n_early:n_col], start=True, stop=True)
        lnz = keep.tile([P, n_col], F32, name="lnz")
        nc.scalar.activation(out=lnz[0:B_HI, :], in_=zs[0:B_HI, 0:n_col], func=ACT.Ln)
        res = keep.tile([P, n_col], F32, name="res")
        nc.vector.tensor_tensor(out=res[0:B_HI, :], in0=lnz[0:B_HI, :], in1=zd[0:B_HI, 0:n_col], op=ALU.subtract)
        for k in range(N_STEP):
            n_s = N_SLICE - k
            g0 = GROUP0[k]
            queue = nc.sync if k % 2 == 0 else nc.scalar
            queue.dma_start(
                out=out[P * g0 : P * (g0 + n_s)].rearrange("(q c) -> q c", q=B_HI),
                in_=res[0:B_HI, B_LO * g0 : B_LO * (g0 + n_s)],
            )
